import numpy as np
import ml_dtypes


def mxq(x, axis, fmt="e4m3"):
    dtype, down = {"e4m3": (ml_dtypes.float8_e4m3fn, 7), "e5m2": (ml_dtypes.float8_e5m2, 14)}[fmt]
    v = np.moveaxis(np.asarray(x, np.float32).astype(ml_dtypes.bfloat16).astype(np.float64), axis, -1)
    blocks = v.reshape(v.shape[:-1] + (-1, 32))
    amax = np.abs(blocks).max(-1, keepdims=True)
    byte = np.maximum(np.where(amax > 0, np.frexp(amax)[1] - 1 + 127, 0) - down, 1)
    scale = np.exp2(byte - 127.0)
    codes = (blocks / scale).astype(np.float32).astype(dtype).astype(np.float64)
    return np.moveaxis((codes * scale).reshape(v.shape), -1, axis)


WIDE = False


def mx_kscale(k):
    if not WIDE:
        return np.ones(k)
    levels = np.array([10, -10, 5, -5, 0])
    if k % 512:
        return np.exp2(np.random.permutation(np.resize(levels, k // 32))).repeat(32)
    a = np.empty((k // 512, 16))
    for p in range(k // 512):
        a[p, :8] = np.random.permutation(np.resize(levels, 8))
        for g in range(8):
            far = levels[np.abs(levels - a[p, g]) >= 10]
            a[p, g + 8] = far[np.random.randint(len(far))]
    return np.exp2(a.ravel()).repeat(32)


BF16 = ml_dtypes.bfloat16


def bf(x):
    return np.asarray(x, np.float32).astype(BF16)


def f64(x):
    return np.asarray(x).astype(np.float64)


B, I, U = 256, 1024, 1024
QR = True


def hard_sigmoid(v):
    return np.clip(0.2 * v + 0.5, 0.0, 1.0)


def rec_mm(a, w):
    if QR:
        return mxq(a, 1, "e4m3") @ mxq(w, 0, "e4m3")
    return a @ w


def draw0():
    s = mx_kscale(I)
    t = mx_kscale(U) if QR else np.ones(U)
    r = mx_kscale(U) if QR else np.ones(U)
    bias = np.random.standard_normal(4 * U) * 0.1
    bias[U:2 * U] += 1.0
    return {"inputs": bf(np.random.standard_normal((B, I)) * s),
            "h_tm1": bf(np.random.standard_normal((B, U)) * t),
            "c_tm1": bf(np.random.standard_normal((B, U))),
            "z_tm1": bf(np.random.standard_normal((B, U)) * r),
            "kernel": bf(np.random.standard_normal((I, 4 * U)) / np.sqrt(I) / s[:, None]),
            "recurrent_kernel": bf(np.random.standard_normal((U, 4 * U)) / np.sqrt(U) / t[:, None]),
            "recurrent_latent": bf(np.random.standard_normal((U, 4 * U)) / np.sqrt(U) / r[:, None]),
            "bias": bf(bias)}


def core(inputs, h_tm1, c_tm1, z_tm1, kernel, recurrent_kernel, recurrent_latent, bias):
    x = (mxq(f64(inputs), 1, "e4m3") @ mxq(f64(kernel), 0, "e4m3")) + rec_mm(f64(h_tm1), f64(recurrent_kernel)) + rec_mm(f64(z_tm1), f64(recurrent_latent)) + f64(bias)
    x_i, x_f, x_c, x_o = np.split(x, 4, axis=1)
    i = hard_sigmoid(x_i)
    f = hard_sigmoid(x_f)
    c = f * f64(c_tm1) + i * np.tanh(x_c)
    o = hard_sigmoid(x_o)
    h = o * np.tanh(c)
    return h


def e4m3fn_bytes(y):
    return np.clip(np.asarray(y, np.float64), -448.0, 448.0).astype(np.float32).astype(ml_dtypes.float8_e4m3fn).view(np.uint8)


def e4m3fn_values(b):
    return np.asarray(b, np.uint8).view(ml_dtypes.float8_e4m3fn).astype(np.float64)


def setup_inputs():
    d = draw0()
    x0 = np.asarray(d['recurrent_latent']).astype(np.float64)
    s = (np.max(np.abs(x0), axis=(1,), keepdims=True) / 448.0).astype(np.float32)
    out = {}
    for k, v in d.items():
        if k == 'recurrent_latent':
            out['recurrent_latent_bytes'] = e4m3fn_bytes(x0 / s.astype(np.float64))
            out['recurrent_latent_scale'] = s
        else:
            out[k] = v
    return out


def reference(inputs, h_tm1, c_tm1, z_tm1, kernel, recurrent_kernel, recurrent_latent_bytes, recurrent_latent_scale, bias):
    return core(inputs, h_tm1, c_tm1, z_tm1, kernel, recurrent_kernel, e4m3fn_values(recurrent_latent_bytes) * recurrent_latent_scale.astype(np.float64), bias)

@@ -1,0 +1,411 @@
+from contextlib import ExitStack
+
+import concourse.masks as masks
+import concourse.mybir as mybir
+
+B, I, U = 256, 1024, 1024
+FLOPS = 2 * B * (I + U + U) * 4 * U
+
+F32 = mybir.dt.float32
+BF16 = mybir.dt.bfloat16
+U32 = mybir.dt.uint32
+U8 = mybir.dt.uint8
+FP8 = mybir.dt.float8_e4m3fn
+FP8X4 = mybir.dt.float8_e4m3fn_x4
+ACT = mybir.ActivationFunctionType
+ALU = mybir.AluOpType
+
+P = 128
+PACK = 4
+D16 = 5
+D8 = 3
+GV = 3
+PE_RUN = 8
+RUN = 4
+GATES = ((2 * U, "c"), (0, "i"), (U, "f"), (3 * U, "o"))
+UNITS = (
+    (0, 0, 1024, (0, 1, 2, 3), ()),
+    (1, 0, 1024, (0, 1, 2, 3), ()),
+    (2, 0, 1024, (0, 1, 2, 3), ()),
+    (3, 0, 512, (0, 1), (6, 7)),
+    (3, 512, 256, (2,), (5, 0)),
+    (3, 768, 256, (3, 4), (1, 2)),
+)
+PE_BANKS = (4, 5, 6, 7)
+VCOLS = 256
+K0, K1, R0, R1, L0, L1 = 0, 1, 2, 3, 4, 5
+S_HELP = (R0, R1)
+
+
+def tile_vlstmcell_kernel(tc, inputs, h_tm1, c_tm1, z_tm1, kernel, recurrent_kernel,
+                                      recurrent_latent_bytes, recurrent_latent_scale, bias, out):
+    nc = tc.nc
+    with ExitStack() as ctx:
+        const = ctx.enter_context(tc.tile_pool(name="const", bufs=1))
+        raw16 = ctx.enter_context(tc.tile_pool(name="raw16", bufs=D16))
+        raw8 = ctx.enter_context(tc.tile_pool(name="raw8", bufs=D8))
+        work = ctx.enter_context(tc.tile_pool(name="work", bufs=2))
+        keep = ctx.enter_context(tc.tile_pool(name="keep", bufs=12))
+        araw = ctx.enter_context(tc.tile_pool(name="araw", bufs=4))
+        psum = ctx.enter_context(tc.psum_pool(name="psum", bufs=1))
+        ctx.enter_context(tc.manual_schedule())
+
+        def bank(i, shape, dtype):
+            return psum.tile(shape, dtype, name="bank%d" % i, tag="bank%d" % i)
+
+        w_views = [w.rearrange("(g p t) n -> g p t n", g=2, p=P, t=PACK)
+                   for w in (kernel, recurrent_kernel, recurrent_latent_bytes)]
+        chunks = [[{"ps": ps, "col": GATES[gt][0]} for ps in range(6)] for gt in range(4)]
+        order16 = [chunks[gt][ps] for gt in range(4) for ps in (K0, K1, R0, R1)]
+        order8 = [chunks[gt][ps] for gt in range(4) for ps in (L0, L1)]
+        st = {"n16": 0, "n8": 0}
+
+        ident_f = const.tile([P, P], F32, name="ident_f")
+        ident_b = const.tile([P, P], BF16, name="ident_b")
+        b_rows = const.tile([P, P], BF16, name="b_rows")
+        warm = const.tile([P, 1], F32, name="warm")
+        sc = const.tile([P, 2, PACK], F32, name="sc")
+        bias_pl = const.tile([P, 32], F32, name="bias_pl")
+        bias_hs = const.tile([P, 32], F32, name="bias_hs")
+        a_codes = const.tile([P, 6, B], U32, name="a_codes", align_bytes=64)
+        a_scl = const.tile([P, 6, B], U8, name="a_scl", align_bytes=64)
+        g_st = const.tile([P, 8, B], F32, name="g_st")
+        c_t = const.tile([P, 8, B], BF16, name="c_t")
+        nc.gpsimd.memset(warm[:], 0.0)
+        nc.scalar.activation(out=warm[:], in_=warm[:], func=ACT.Tanh)
+        masks.make_identity(nc, ident_b[:])
+        masks.make_identity(nc, ident_f[:])
+        nc.gpsimd.memset(b_rows[:], 0.0)
+
+        def load(ch, pieces=1, planes=False):
+            s, g = divmod(ch["ps"], 2)
+            col = ch["col"]
+            if s == 2:
+                raw = raw8.tile([P, PACK, U], U8, name="raw8")
+            else:
+                raw = raw16.tile([P, PACK, U], BF16, name="raw16")
+            ch["raw"] = raw
+            ch["src"] = raw
+            todo = []
+            if planes:
+                for t in range(PACK):
+                    todo.append((raw[:, t, :], w_views[s][g][:, t, col:col + U]))
+            else:
+                step = U // pieces
+                for a in range(0, U, step):
+                    todo.append((raw[:, :, a:a + step], w_views[s][g][:, :, col + a:col + a + step]))
+            return todo
+
+        def dma(pairs):
+            for o, i in pairs:
+                nc.sync.dma_start(out=o, in_=i)
+
+        def next16():
+            if st["n16"] < len(order16):
+                dma(load(order16[st["n16"]]))
+                st["n16"] += 1
+
+        def next8():
+            if st["n8"] < len(order8):
+                dma(load(order8[st["n8"]]))
+                st["n8"] += 1
+
+        def widen(ch):
+            g = ch["ps"] % 2
+            wide = work.tile([P, PACK, U], BF16, name="wide")
+            for t in range(PACK):
+                nc.scalar.activation(out=wide[:, t, :], in_=ch["raw"][:, t, :].bitcast(FP8), func=ACT.Copy,
+                                     scale=sc[:, g, t:t + 1])
+            ch["src"] = wide
+            next8()
+
+        def interleave(eng, grp, ch, c0, c1):
+            o = grp
+            i = ch["src"][:, :, c0:c1]
+            if RUN:
+                o = o.rearrange("p (c i) t -> p c t i", i=RUN)
+                i = i.rearrange("p t (c i) -> p c t i", i=RUN)
+            else:
+                i = i.rearrange("p t c -> p c t")
+            if eng == "V":
+                nc.vector.tensor_copy(out=o, in_=i)
+            else:
+                nc.scalar.copy(out=o, in_=i)
+
+        def pe_fill(ch, b):
+            pb = bank(PE_BANKS[b], [P, 256, PACK], BF16)
+            for h in range(2):
+                c0 = 256 * b + 128 * h
+                nc.tensor.matmul(out=pb[:, 128 * h:128 * h + 128, :].rearrange("p (c i) t -> p c t i", i=PE_RUN), lhsT=ident_b[:],
+                                 rhs=ch["src"][:, :, c0:c0 + 128].rearrange("p t (c i) -> p c t i", i=PE_RUN),
+                                 start=True, stop=True)
+            ch["pb%d" % b] = pb
+
+        def pe_drain(ch, b):
+            nc.scalar.copy(out=ch["grp"][:, 256 * b:256 * b + 256, :], in_=ch["pb%d" % b][:])
+
+        codes = {}
+
+        def quantize(u, ps, grp):
+            gt, c0, w = UNITS[u][0], UNITS[u][1], UNITS[u][2]
+            if (gt, ps) not in codes:
+                codes[(gt, ps)] = (keep.tile([P, U], U32, name="codes", align_bytes=64),
+                                   keep.tile([P, U], U8, name="scl", align_bytes=64))
+            cd, sl = codes[(gt, ps)]
+            nc.vector.quantize_mx(out=cd[:, c0:c0 + w].bitcast(FP8X4), scales=sl[:, c0:c0 + w],
+                                  in_=grp.rearrange("p c t -> p (c t)"))
+
+        def mx(acc, u, ps, jj, start, stop):
+            cd, sl = codes[(UNITS[u][0], ps)]
+            c = UNITS[u][1] + P * jj
+            nc.tensor.matmul_mx(out=acc, lhsT=cd[:, c:c + P].bitcast(FP8X4), lhsT_scale=sl[:, c:c + P],
+                                rhs=a_codes[:, ps, :].bitcast(FP8X4), rhs_scale=a_scl[:, ps, :], start=start, stop=stop)
+
+        accs = {}
+
+        def mm_unit(u):
+            for jj in range(UNITS[u][2] // P):
+                if jj % 2 == 0:
+                    bk = bank(UNITS[u][3][jj // 2], [P, 2, B], F32)
+                accs[(u, jj)] = bk[:, jj % 2, :]
+                for ps in range(6):
+                    mx(accs[(u, jj)], u, ps, jj, ps == 0, ps == 5)
+
+        rt = {}
+
+        def kind(u):
+            return GATES[UNITS[u][0]][1]
+
+        def read_gate(u, jj, eng):
+            j = UNITS[u][1] // P + jj
+            col = GATES[UNITS[u][0]][0] // P + j
+            if kind(u) == "c":
+                nc.scalar.activation(out=g_st[:, j, :], in_=accs[(u, jj)], func=ACT.Tanh,
+                                     bias=bias_pl[:, col:col + 1], scale=1.0)
+            elif eng == "S":
+                nc.scalar.activation(out=rt[u][:, jj, :], in_=accs[(u, jj)], func=ACT.Relu,
+                                     bias=bias_hs[:, col:col + 1], scale=1.0)
+            else:
+                nc.vector.tensor_scalar(out=rt[u][:, jj, :], in0=accs[(u, jj)], scalar1=bias_hs[:, col:col + 1],
+                                        scalar2=0.0, op0=ALU.add, op1=ALU.max)
+
+        def fl(ap):
+            return ap.rearrange("p j b -> p (j b)")
+
+        def clip_mul(o, r, other):
+            nc.vector.scalar_tensor_tensor(out=fl(o), in0=fl(r), scalar=5.0, in1=fl(other), op0=ALU.min, op1=ALU.mult)
+
+        def r_tile(u):
+            nt = UNITS[u][2] // P
+            rt[u] = work.tile([P, nt, B], F32, name="r%d" % nt, bufs=(2 if nt == 2 else 1))
+
+        def after_s(u):
+            if kind(u) != "c":
+                r_tile(u)
+            for jj in range(UNITS[u][2] // P):
+                read_gate(u, jj, "S")
+
+        def after_v(u):
+            if kind(u) == "i":
+                clip_mul(g_st[:], rt[u][:], g_st[:])
+            elif kind(u) == "f":
+                clip_mul(rt[u][:], rt[u][:], c_t[:])
+                nc.vector.tensor_tensor(out=fl(g_st[:]), in0=fl(g_st[:]), in1=fl(rt[u][:]), op=ALU.add)
+
+        tps = {}
+
+        def o_stt(u):
+            j0, nt = UNITS[u][1] // P, UNITS[u][2] // P
+            clip_mul(rt[u][:], rt[u][:], g_st[:, j0:j0 + nt, :])
+
+        def o_tr(u):
+            nt = UNITS[u][2] // P
+            for a in range(2):
+                tp = bank(UNITS[u][4][a], [P, nt * P], F32)
+                for jj in range(nt):
+                    nc.tensor.transpose(tp[:, P * jj:P * jj + P], rt[u][:, jj, P * a:P * a + P], ident_f[:])
+                tps[(u, a)] = tp
+
+        def o_out(u, ost, engs):
+            c0, w = UNITS[u][1], UNITS[u][2]
+            for a in range(2):
+                if engs[a] == "S":
+                    nc.scalar.activation(out=ost[:, a, :], in_=tps[(u, a)][:], func=ACT.Copy, scale=0.2)
+                else:
+                    nc.vector.tensor_scalar(out=ost[:, a, :], in0=tps[(u, a)][:], scalar1=0.2, scalar2=None, op0=ALU.mult)
+            nc.sync.dma_start(out=out.rearrange("(a p) n -> p a n", a=2)[:, :, c0:c0 + w], in_=ost)
+
+        nc.sync.dma_start(out=sc[:], in_=recurrent_latent_scale.rearrange("(g p t) o -> p g (t o)", g=2, p=P, t=PACK))
+        first16 = load(order16[0], pieces=4)
+        first8 = load(order8[0], planes=True)
+        st["n16"], st["n8"] = 1, 1
+        for n in range(4):
+            dma([first16[n], first8[n]])
+        next16()
+        next8()
+        next16()
+        next16()
+        acts = []
+        for x in (inputs, h_tm1, z_tm1, c_tm1):
+            xa = araw.tile([P, 2, I], BF16, name="araw")
+            nc.sync.dma_start(out=xa[:], in_=x.rearrange("(a p) k -> p a k", a=2))
+            acts.append(xa)
+        nc.sync.dma_start(out=b_rows[0:32, :], in_=bias.rearrange("(r c) -> r c", c=P))
+        next16()
+        next8()
+
+        def act_prep():
+            for s in range(3):
+                words = acts[s][:].bitcast(F32)
+                agrp = work.tile([P, 2, B, PACK], BF16, name="agrp", align_bytes=64)
+                for g in range(2):
+                    xt = bank((2 * s + g) % 4, [P, 2, B], F32)
+                    for a in range(2):
+                        for u2 in range(2):
+                            nc.tensor.transpose(xt[:, u2, P * a:P * a + P], words[:, a, 256 * g + u2:256 * (g + 1):2], ident_f[:])
+                    nc.scalar.copy(out=agrp[:, g, :, :].bitcast(F32), in_=xt[:].rearrange("p u r -> p r u"))
+                nc.vector.quantize_mx(out=a_codes[:, 2 * s:2 * s + 2, :].rearrange("p g r -> p (g r)").bitcast(FP8X4),
+                                      scales=a_scl[:, 2 * s:2 * s + 2, :].rearrange("p g r -> p (g r)"),
+                                      in_=agrp[:].rearrange("p g r t -> p (g r t)"))
+            for hb in range(2):
+                ctp = bank(6 + hb, [P, 4, B], BF16)
+                for jj in range(4):
+                    for a in range(2):
+                        j = 4 * hb + jj
+                        nc.tensor.transpose(ctp[:, jj, P * a:P * a + P], acts[3][:, a, P * j:P * j + P], ident_b[:])
+                nc.scalar.copy(out=c_t[:, 4 * hb:4 * hb + 4, :], in_=ctp[:])
+            bt = bank(4, [P, P], BF16)
+            nc.tensor.transpose(bt[:], b_rows[:], ident_b[:])
+            nc.vector.tensor_copy(out=bias_pl[:], in_=bt[:, 0:32])
+            nc.vector.tensor_scalar(out=bias_hs[:], in0=bt[:, 0:32], scalar1=2.5, scalar2=None, op0=ALU.add)
+
+        grp16 = {}
+
+        def grp_of(u, ps):
+            c0, w = UNITS[u][1], UNITS[u][2]
+            if ps in (L0, L1):
+                return chunks[UNITS[u][0]][ps]["grp"][:, c0:c0 + w, :]
+            return grp16[(u, ps)][:]
+
+        def il(u, ps, eng="V", tag="grpV"):
+            gt, c0, w = UNITS[u][0], UNITS[u][1], UNITS[u][2]
+            t = work.tile([P, w, PACK], BF16, name=tag, align_bytes=64, bufs=(GV if tag == "grpV" else 2))
+            grp16[(u, ps)] = t
+            if u == 0 and ps == K0:
+                for n in range(4):
+                    interleave(eng, t[:, 256 * n:256 * n + 256, :], chunks[gt][ps], 256 * n, 256 * n + 256)
+            else:
+                interleave(eng, t[:], chunks[gt][ps], c0, c0 + w)
+            if c0 + w == U:
+                next16()
+
+        def q(u, ps):
+            quantize(u, ps, grp_of(u, ps))
+
+        def latent_tile(ch):
+            ch["grp"] = work.tile([P, U, PACK], BF16, name="grpS", align_bytes=64)
+
+        def il_latent(eng, ch, c0, c1):
+            interleave(eng, ch["grp"][:, c0:c1, :], ch, c0, c1)
+
+        for u in range(3):
+            ck = chunks[u]
+            il(u, K0)
+            if u > 0:
+                q(u - 1, L1)
+                mm_unit(u - 1)
+            widen(ck[L0])
+            widen(ck[L1])
+            latent_tile(ck[L0])
+            latent_tile(ck[L1])
+            for b in range(4):
+                pe_fill(ck[L1], b)
+            il_latent("S", ck[L0], VCOLS, U)
+            if u > 0:
+                after_s(u - 1)
+            for b in range(4):
+                pe_drain(ck[L1], b)
+            if u == 0:
+                q(u, K0)
+                il(u, K1)
+            else:
+                il(u, K1)
+                q(u, K0)
+            il(u, R0)
+            q(u, K1)
+            il(u, R1)
+            q(u, R0)
+            il_latent("V", ck[L0], 0, VCOLS)
+            q(u, R1)
+            q(u, L0)
+            if u == 0:
+                act_prep()
+            else:
+                after_v(u - 1)
+
+        ck = chunks[3]
+        il(3, K0)
+        q(2, L1)
+        mm_unit(2)
+        widen(ck[L0])
+        latent_tile(ck[L0])
+        il_latent("S", ck[L0], VCOLS, U)
+        after_s(2)
+        widen(ck[L1])
+        latent_tile(ck[L1])
+        for b in range(4):
+            pe_fill(ck[L1], b)
+        il(3, K1)
+        q(3, K0)
+        il(3, R0)
+        q(3, K1)
+        il(3, R1)
+        q(3, R0)
+        il_latent("V", ck[L0], 0, VCOLS)
+        q(3, R1)
+        il(4, K0)
+        il(4, K1)
+        q(4, K0)
+        il(4, R0)
+        q(4, K1)
+        il(4, R1)
+        q(4, R0)
+        q(4, R1)
+        q(3, L0)
+        after_v(2)
+        for ps in S_HELP:
+            il(5, ps, "S", "grpH")
+        for b in range(4):
+            pe_drain(ck[L1], b)
+        nc.scalar.activation(out=fl(g_st[:]), in_=fl(g_st[:]), func=ACT.Tanh, scale=0.2)
+        q(3, L1)
+        mm_unit(3)
+        q(4, L0)
+        q(4, L1)
+        mm_unit(4)
+        after_s(3)
+        after_s(4)
+        for jj in range(2):
+            accs[(5, jj)] = bank(UNITS[5][3][jj], [P, B], F32)[:]
+        for ps in (K0, K1, R0, R1):
+            if ps not in S_HELP:
+                il(5, ps)
+        passes = (K0, K1, L0, L1, R0, R1)
+        for n, ps in enumerate(passes):
+            if n == 5:
+                o_stt(3)
+            q(5, ps)
+            for jj in range(2):
+                mx(accs[(5, jj)], 5, ps, jj, n == 0, n == 5)
+        o_tr(3)
+        o_stt(4)
+        o_tr(4)
+        r_tile(5)
+        read_gate(5, 0, "S")
+        read_gate(5, 1, "V")
+        o_stt(5)
+        o_tr(5)
+        o_out(3, work.tile([P, 2, 4 * P], F32, name="agrp", align_bytes=64)[:], "SS")
+        ost = work.tile([P, 2, 2, 2 * P], F32, name="agrp", align_bytes=64)
+        o_out(4, ost[:, 0, :, :], "SV")
+        o_out(5, ost[:, 1, :, :], "SV")

@@ -23,18 +23,11 @@ GV = 3
 PE_RUN = 8
 RUN = 4
 GATES = ((2 * U, "c"), (0, "i"), (U, "f"), (3 * U, "o"))
-UNITS = (
-    (0, 0, 1024, (0, 1, 2, 3), ()),
-    (1, 0, 1024, (0, 1, 2, 3), ()),
-    (2, 0, 1024, (0, 1, 2, 3), ()),
-    (3, 0, 512, (0, 1), (6, 7)),
-    (3, 512, 256, (2,), (5, 0)),
-    (3, 768, 256, (3, 4), (1, 2)),
-)
-PE_BANKS = (4, 5, 6, 7)
-VCOLS = 256
+UNITS = ((0, 0, 1024), (1, 0, 1024), (2, 0, 1024), (3, 0, 512), (3, 512, 256), (3, 768, 256))
+VC = (128, 128, 128, 128)
+PC = (256, 256, 256, 0)
+V_WIDENS = True
 K0, K1, R0, R1, L0, L1 = 0, 1, 2, 3, 4, 5
-S_HELP = (R0, R1)
 
 
 def tile_vlstmcell_kernel(tc, inputs, h_tm1, c_tm1, z_tm1, kernel, recurrent_kernel,
@@ -57,7 +50,7 @@ def tile_vlstmcell_kernel(tc, inputs, h_tm1, c_tm1, z_tm1, kernel, recurrent_ker
                    for w in (kernel, recurrent_kernel, recurrent_latent_bytes)]
         chunks = [[{"ps": ps, "col": GATES[gt][0]} for ps in range(6)] for gt in range(4)]
         order16 = [chunks[gt][ps] for gt in range(4) for ps in (K0, K1, R0, R1)]
-        order8 = [chunks[gt][ps] for gt in range(4) for ps in (L0, L1)]
+        order8 = [chunks[0][L0], chunks[0][L1]] + [chunks[gt][ps] for gt in range(1, 4) for ps in (L1, L0)]
         st = {"n16": 0, "n8": 0}
 
         ident_f = const.tile([P, P], F32, name="ident_f")
@@ -110,44 +103,48 @@ def tile_vlstmcell_kernel(tc, inputs, h_tm1, c_tm1, z_tm1, kernel, recurrent_ker
                 dma(load(order8[st["n8"]]))
                 st["n8"] += 1
 
-        def widen(ch):
+        def wide_tile(ch):
+            ch["src"] = work.tile([P, PACK, U], BF16, name="wide")
+
+        def widen_plane(ch, t, eng):
             g = ch["ps"] % 2
-            wide = work.tile([P, PACK, U], BF16, name="wide")
-            for t in range(PACK):
-                nc.scalar.activation(out=wide[:, t, :], in_=ch["raw"][:, t, :].bitcast(FP8), func=ACT.Copy,
+            if eng == "S":
+                nc.scalar.activation(out=ch["src"][:, t, :], in_=ch["raw"][:, t, :].bitcast(FP8), func=ACT.Copy,
                                      scale=sc[:, g, t:t + 1])
-            ch["src"] = wide
+            else:
+                nc.vector.tensor_scalar(out=ch["src"][:, t, :], in0=ch["raw"][:, t, :].bitcast(FP8), scalar1=sc[:, g, t:t + 1],
+                                        scalar2=None, op0=ALU.mult)
+
+        def widen(ch):
+            wide_tile(ch)
+            for t in range(PACK):
+                widen_plane(ch, t, "S")
             next8()
 
         def interleave(eng, grp, ch, c0, c1):
-            o = grp
-            i = ch["src"][:, :, c0:c1]
-            if RUN:
-                o = o.rearrange("p (c i) t -> p c t i", i=RUN)
-                i = i.rearrange("p t (c i) -> p c t i", i=RUN)
-            else:
-                i = i.rearrange("p t c -> p c t")
+            o = grp.rearrange("p (c i) t -> p c t i", i=RUN)
+            i = ch["src"][:, :, c0:c1].rearrange("p t (c i) -> p c t i", i=RUN)
             if eng == "V":
                 nc.vector.tensor_copy(out=o, in_=i)
             else:
                 nc.scalar.copy(out=o, in_=i)
 
-        def pe_fill(ch, b):
-            pb = bank(PE_BANKS[b], [P, 256, PACK], BF16)
+        def fill(ch, c0, b):
+            pb = bank(b, [P, 256, PACK], BF16)
             for h in range(2):
-                c0 = 256 * b + 128 * h
+                c = c0 + 128 * h
                 nc.tensor.matmul(out=pb[:, 128 * h:128 * h + 128, :].rearrange("p (c i) t -> p c t i", i=PE_RUN), lhsT=ident_b[:],
-                                 rhs=ch["src"][:, :, c0:c0 + 128].rearrange("p t (c i) -> p c t i", i=PE_RUN),
+                                 rhs=ch["src"][:, :, c:c + 128].rearrange("p t (c i) -> p c t i", i=PE_RUN),
                                  start=True, stop=True)
-            ch["pb%d" % b] = pb
+            ch["pb%d" % c0] = pb
 
-        def pe_drain(ch, b):
-            nc.scalar.copy(out=ch["grp"][:, 256 * b:256 * b + 256, :], in_=ch["pb%d" % b][:])
+        def drain(ch, c0):
+            nc.scalar.copy(out=ch["grp"][:, c0:c0 + 256, :], in_=ch["pb%d" % c0][:])
 
         codes = {}
 
         def quantize(u, ps, grp):
-            gt, c0, w = UNITS[u][0], UNITS[u][1], UNITS[u][2]
+            gt, c0, w = UNITS[u]
             if (gt, ps) not in codes:
                 codes[(gt, ps)] = (keep.tile([P, U], U32, name="codes", align_bytes=64),
                                    keep.tile([P, U], U8, name="scl", align_bytes=64))
@@ -163,10 +160,10 @@ def tile_vlstmcell_kernel(tc, inputs, h_tm1, c_tm1, z_tm1, kernel, recurrent_ker
 
         accs = {}
 
-        def mm_unit(u):
+        def mm_unit(u, banks):
             for jj in range(UNITS[u][2] // P):
                 if jj % 2 == 0:
-                    bk = bank(UNITS[u][3][jj // 2], [P, 2, B], F32)
+                    bk = bank(banks[jj // 2], [P, 2, B], F32)
                 accs[(u, jj)] = bk[:, jj % 2, :]
                 for ps in range(6):
                     mx(accs[(u, jj)], u, ps, jj, ps == 0, ps == 5)
@@ -176,108 +173,120 @@ def tile_vlstmcell_kernel(tc, inputs, h_tm1, c_tm1, z_tm1, kernel, recurrent_ker
         def kind(u):
             return GATES[UNITS[u][0]][1]
 
-        def read_gate(u, jj, eng):
+        def read_gate(u, jj):
             j = UNITS[u][1] // P + jj
             col = GATES[UNITS[u][0]][0] // P + j
             if kind(u) == "c":
                 nc.scalar.activation(out=g_st[:, j, :], in_=accs[(u, jj)], func=ACT.Tanh,
                                      bias=bias_pl[:, col:col + 1], scale=1.0)
-            elif eng == "S":
-                nc.scalar.activation(out=rt[u][:, jj, :], in_=accs[(u, jj)], func=ACT.Relu,
-                                     bias=bias_hs[:, col:col + 1], scale=1.0)
             else:
-                nc.vector.tensor_scalar(out=rt[u][:, jj, :], in0=accs[(u, jj)], scalar1=bias_hs[:, col:col + 1],
-                                        scalar2=0.0, op0=ALU.add, op1=ALU.max)
+                nc.scalar.activation(out=rt[u][:, jj, :], in_=accs[(u, jj)], func=ACT.Relu,
+                                     bias=bias_hs[:, col:col + 1], scale=0.2)
 
         def fl(ap):
             return ap.rearrange("p j b -> p (j b)")
 
         def clip_mul(o, r, other):
-            nc.vector.scalar_tensor_tensor(out=fl(o), in0=fl(r), scalar=5.0, in1=fl(other), op0=ALU.min, op1=ALU.mult)
+            nc.vector.scalar_tensor_tensor(out=fl(o), in0=fl(r), scalar=1.0, in1=fl(other), op0=ALU.min, op1=ALU.mult)
 
-        def r_tile(u):
+        def read_unit(u):
             nt = UNITS[u][2] // P
-            rt[u] = work.tile([P, nt, B], F32, name="r%d" % nt, bufs=(2 if nt == 2 else 1))
-
-        def after_s(u):
             if kind(u) != "c":
-                r_tile(u)
-            for jj in range(UNITS[u][2] // P):
-                read_gate(u, jj, "S")
+                rt[u] = work.tile([P, nt, B], F32, name="r%d" % nt, bufs=(2 if nt == 2 else 1))
+            for jj in range(nt):
+                read_gate(u, jj)
 
-        def after_v(u):
-            if kind(u) == "i":
-                clip_mul(g_st[:], rt[u][:], g_st[:])
-            elif kind(u) == "f":
-                clip_mul(rt[u][:], rt[u][:], c_t[:])
-                nc.vector.tensor_tensor(out=fl(g_st[:]), in0=fl(g_st[:]), in1=fl(rt[u][:]), op=ALU.add)
+        def c_sum(bks):
+            cbs = []
+            for a in range(2):
+                for h in range(2):
+                    cb = bank(bks[2 * a + h], [P, 4, P], F32)
+                    for jj in range(4):
+                        j = 4 * h + jj
+                        nc.tensor.matmul(out=cb[:, jj, :], lhsT=g_st[:, j, P * a:P * a + P], rhs=ident_f[:], is_transpose=True,
+                                         start=True, stop=False)
+                        nc.tensor.matmul(out=cb[:, jj, :], lhsT=rt[2][:, j, P * a:P * a + P], rhs=ident_f[:], is_transpose=True,
+                                         start=False, stop=True)
+                    cbs.append(cb)
+            return cbs
+
+        def c_tanh(cbs):
+            th = work.tile([P, 2, U], F32, name="r8", bufs=1)
+            for a in range(2):
+                for h in range(2):
+                    nc.scalar.activation(out=th[:, a, 512 * h:512 * h + 512], in_=cbs[2 * a + h][:].rearrange("p j n -> p (j n)"),
+                                         func=ACT.Tanh)
+            return th
 
         tps = {}
 
-        def o_stt(u):
-            j0, nt = UNITS[u][1] // P, UNITS[u][2] // P
-            clip_mul(rt[u][:], rt[u][:], g_st[:, j0:j0 + nt, :])
-
-        def o_tr(u):
+        def o_tr(u, bks):
             nt = UNITS[u][2] // P
             for a in range(2):
-                tp = bank(UNITS[u][4][a], [P, nt * P], F32)
+                if len(bks) == 2:
+                    tp = bank(bks[a], [P, nt * P], F32)[:]
+                else:
+                    if a == 0:
+                        both = bank(bks[0], [P, 2, nt * P], F32)
+                    tp = both[:, a, :]
                 for jj in range(nt):
                     nc.tensor.transpose(tp[:, P * jj:P * jj + P], rt[u][:, jj, P * a:P * a + P], ident_f[:])
                 tps[(u, a)] = tp
+            if len(bks) == 1:
+                tps[u] = both
 
-        def o_out(u, ost, engs):
+        def o_out(u, ost, th):
             c0, w = UNITS[u][1], UNITS[u][2]
-            for a in range(2):
-                if engs[a] == "S":
-                    nc.scalar.activation(out=ost[:, a, :], in_=tps[(u, a)][:], func=ACT.Copy, scale=0.2)
-                else:
-                    nc.vector.tensor_scalar(out=ost[:, a, :], in0=tps[(u, a)][:], scalar1=0.2, scalar2=None, op0=ALU.mult)
+            if u in tps:
+                nc.vector.scalar_tensor_tensor(out=ost, in0=tps[u][:], scalar=1.0, in1=th[:, :, c0:c0 + w], op0=ALU.min, op1=ALU.mult)
+            else:
+                for a in range(2):
+                    nc.vector.scalar_tensor_tensor(out=ost[:, a, :], in0=tps[(u, a)], scalar=1.0, in1=th[:, a, c0:c0 + w],
+                                                   op0=ALU.min, op1=ALU.mult)
             nc.sync.dma_start(out=out.rearrange("(a p) n -> p a n", a=2)[:, :, c0:c0 + w], in_=ost)
 
-        nc.sync.dma_start(out=sc[:], in_=recurrent_latent_scale.rearrange("(g p t) o -> p g (t o)", g=2, p=P, t=PACK))
-        first16 = load(order16[0], pieces=4)
-        first8 = load(order8[0], planes=True)
-        st["n16"], st["n8"] = 1, 1
-        for n in range(4):
-            dma([first16[n], first8[n]])
-        next16()
-        next8()
-        next16()
-        next16()
         acts = []
-        for x in (inputs, h_tm1, z_tm1, c_tm1):
-            xa = araw.tile([P, 2, I], BF16, name="araw")
+
+        def act_load(x):
+            xa = araw.tile([P, 2, I], BF16, name="araw", align_bytes=64)
             nc.sync.dma_start(out=xa[:], in_=x.rearrange("(a p) k -> p a k", a=2))
             acts.append(xa)
-        nc.sync.dma_start(out=b_rows[0:32, :], in_=bias.rearrange("(r c) -> r c", c=P))
-        next16()
-        next8()
 
-        def act_prep():
-            for s in range(3):
-                words = acts[s][:].bitcast(F32)
-                agrp = work.tile([P, 2, B, PACK], BF16, name="agrp", align_bytes=64)
-                for g in range(2):
-                    xt = bank((2 * s + g) % 4, [P, 2, B], F32)
-                    for a in range(2):
-                        for u2 in range(2):
-                            nc.tensor.transpose(xt[:, u2, P * a:P * a + P], words[:, a, 256 * g + u2:256 * (g + 1):2], ident_f[:])
-                    nc.scalar.copy(out=agrp[:, g, :, :].bitcast(F32), in_=xt[:].rearrange("p u r -> p r u"))
-                nc.vector.quantize_mx(out=a_codes[:, 2 * s:2 * s + 2, :].rearrange("p g r -> p (g r)").bitcast(FP8X4),
-                                      scales=a_scl[:, 2 * s:2 * s + 2, :].rearrange("p g r -> p (g r)"),
-                                      in_=agrp[:].rearrange("p g r t -> p (g r t)"))
+        agrps = {}
+
+        def act_turn(s):
+            words = acts[s][:].bitcast(F32)
+            agrp = work.tile([P, 2, B, PACK], BF16, name="agrp", align_bytes=64, bufs=3)
+            for g in range(2):
+                xt = bank((2 * s + g) % 3, [P, 2, B], F32)
+                for a in range(2):
+                    for u2 in range(2):
+                        nc.tensor.transpose(xt[:, u2, P * a:P * a + P], words[:, a, 256 * g + u2:256 * (g + 1):2], ident_f[:])
+                nc.scalar.copy(out=agrp[:, g, :, :].bitcast(F32), in_=xt[:].rearrange("p u r -> p r u"))
+            agrps[s] = agrp
+
+        def act_q(s):
+            nc.vector.quantize_mx(out=a_codes[:, 2 * s:2 * s + 2, :].rearrange("p g r -> p (g r)").bitcast(FP8X4),
+                                  scales=a_scl[:, 2 * s:2 * s + 2, :].rearrange("p g r -> p (g r)"),
+                                  in_=agrps[s][:].rearrange("p g r t -> p (g r t)"))
+
+        def c_turn():
             for hb in range(2):
-                ctp = bank(6 + hb, [P, 4, B], BF16)
+                ctp = bank(hb, [P, 4, B], BF16)
                 for jj in range(4):
                     for a in range(2):
                         j = 4 * hb + jj
                         nc.tensor.transpose(ctp[:, jj, P * a:P * a + P], acts[3][:, a, P * j:P * j + P], ident_b[:])
                 nc.scalar.copy(out=c_t[:, 4 * hb:4 * hb + 4, :], in_=ctp[:])
-            bt = bank(4, [P, P], BF16)
+
+        def bias_turn():
+            bt = bank(2, [P, P], BF16)
             nc.tensor.transpose(bt[:], b_rows[:], ident_b[:])
+            return bt
+
+        def bias_out(bt):
             nc.vector.tensor_copy(out=bias_pl[:], in_=bt[:, 0:32])
-            nc.vector.tensor_scalar(out=bias_hs[:], in0=bt[:, 0:32], scalar1=2.5, scalar2=None, op0=ALU.add)
+            nc.vector.tensor_scalar(out=bias_hs[:], in0=bt[:, 0:32], scalar1=0.2, scalar2=0.5, op0=ALU.mult, op1=ALU.add)
 
         grp16 = {}
 
@@ -287,125 +296,190 @@ def tile_vlstmcell_kernel(tc, inputs, h_tm1, c_tm1, z_tm1, kernel, recurrent_ker
                 return chunks[UNITS[u][0]][ps]["grp"][:, c0:c0 + w, :]
             return grp16[(u, ps)][:]
 
-        def il(u, ps, eng="V", tag="grpV"):
-            gt, c0, w = UNITS[u][0], UNITS[u][1], UNITS[u][2]
-            t = work.tile([P, w, PACK], BF16, name=tag, align_bytes=64, bufs=(GV if tag == "grpV" else 2))
-            grp16[(u, ps)] = t
-            if u == 0 and ps == K0:
-                for n in range(4):
-                    interleave(eng, t[:, 256 * n:256 * n + 256, :], chunks[gt][ps], 256 * n, 256 * n + 256)
+        def il(u, ps, eng="V", pieces=1):
+            gt, c0, w = UNITS[u]
+            if eng == "V":
+                t = work.tile([P, w, PACK], BF16, name="grpV", align_bytes=64, bufs=GV)
             else:
-                interleave(eng, t[:], chunks[gt][ps], c0, c0 + w)
-            if c0 + w == U:
+                t = araw.tile([P, w, PACK], BF16, name="araw", align_bytes=64)
+            grp16[(u, ps)] = t
+            return t
+
+        def il_go(u, ps, eng="V", part=None):
+            gt, c0, w = UNITS[u]
+            t = grp16[(u, ps)]
+            a, b = part or (0, w)
+            interleave(eng, t[:, a:b, :], chunks[gt][ps], c0 + a, c0 + b)
+            if c0 + b == U:
                 next16()
 
-        def q(u, ps):
+        def IL(u, ps, eng="V"):
+            il(u, ps, eng)
+            il_go(u, ps, eng)
+
+        def Q(u, ps):
             quantize(u, ps, grp_of(u, ps))
 
         def latent_tile(ch):
             ch["grp"] = work.tile([P, U, PACK], BF16, name="grpS", align_bytes=64)
 
         def il_latent(eng, ch, c0, c1):
-            interleave(eng, ch["grp"][:, c0:c1, :], ch, c0, c1)
+            if c1 > c0:
+                interleave(eng, ch["grp"][:, c0:c1, :], ch, c0, c1)
 
-        for u in range(3):
-            ck = chunks[u]
-            il(u, K0)
-            if u > 0:
-                q(u - 1, L1)
-                mm_unit(u - 1)
-            widen(ck[L0])
-            widen(ck[L1])
-            latent_tile(ck[L0])
+        def fill_l1(gt):
+            for b in range(4):
+                fill(chunks[gt][L1], 256 * b, 4 + b)
+
+        def produce_b(gt):
+            ck = chunks[gt]
             latent_tile(ck[L1])
+            latent_tile(ck[L0])
+            if PC[gt]:
+                fill(ck[L0], U - PC[gt], 3)
+            if gt == 0:
+                il_latent("S", ck[L0], VC[gt], U - PC[gt])
             for b in range(4):
-                pe_fill(ck[L1], b)
-            il_latent("S", ck[L0], VCOLS, U)
-            if u > 0:
-                after_s(u - 1)
-            for b in range(4):
-                pe_drain(ck[L1], b)
-            if u == 0:
-                q(u, K0)
-                il(u, K1)
-            else:
-                il(u, K1)
-                q(u, K0)
-            il(u, R0)
-            q(u, K1)
-            il(u, R1)
-            q(u, R0)
-            il_latent("V", ck[L0], 0, VCOLS)
-            q(u, R1)
-            q(u, L0)
-            if u == 0:
-                act_prep()
-            else:
-                after_v(u - 1)
+                drain(ck[L1], 256 * b)
+            if PC[gt]:
+                drain(ck[L0], U - PC[gt])
+            if gt > 0:
+                il_latent("S", ck[L0], VC[gt], U - PC[gt])
 
+        ck = chunks[0]
+        nc.sync.dma_start(out=sc[:], in_=recurrent_latent_scale.rearrange("(g p t) o -> p g (t o)", g=2, p=P, t=PACK))
+        first16 = load(order16[0], pieces=4)
+        l0p = load(order8[0], planes=True)
+        l1p = load(order8[1], planes=True)
+        st["n16"], st["n8"] = 1, 2
+        for n in range(4):
+            dma([l0p[n], l1p[n], first16[n]])
+        next16()
+        next8()
+        next16()
+        wide_tile(ck[L0])
+        wide_tile(ck[L1])
+        il(0, K0)
+        for n in range(4):
+            widen_plane(ck[L0], n, "S")
+            widen_plane(ck[L1], n, "V" if V_WIDENS else "S")
+            il_go(0, K0, "V", (256 * n, 256 * n + 256))
+        next8()
+        next16()
+        act_load(inputs)
+        act_load(h_tm1)
+        next16()
+        act_load(z_tm1)
+        act_load(c_tm1)
+        nc.sync.dma_start(out=b_rows[0:32, :], in_=bias.rearrange("(r c) -> r c", c=P))
+        next8()
+        fill_l1(0)
+        produce_b(0)
+        il_latent("V", ck[L0], 0, VC[0])
+        Q(0, K0)
+        IL(0, K1)
+        IL(0, R0)
+        Q(0, K1)
+        IL(0, R1)
+        Q(0, R0)
+        Q(0, L1)
+        Q(0, R1)
+        Q(0, L0)
+
+        widen(chunks[1][L1])
+        fill_l1(1)
+        widen(chunks[1][L0])
+        for s in range(3):
+            act_turn(s)
+        c_turn()
+        bt = bias_turn()
+        produce_b(1)
+        il_latent("V", chunks[1][L0], 0, VC[1])
+        widen(chunks[2][L1])
+        IL(1, K0)
+        act_q(0)
+        act_q(1)
+        IL(1, K1)
+        Q(1, K0)
+        act_q(2)
+        bias_out(bt)
+        mm_unit(0, (0, 1, 2, 3))
+        fill_l1(2)
+        read_unit(0)
+        widen(chunks[2][L0])
+        IL(1, R0)
+        Q(1, K1)
+        IL(1, R1)
+        Q(1, R0)
+        Q(1, R1)
+        Q(1, L1)
+        Q(1, L0)
+
+        produce_b(2)
+        widen(chunks[3][L1])
+        mm_unit(1, (0, 1, 2, 3))
+        fill_l1(3)
+        read_unit(1)
+        IL(2, K0)
+        IL(2, K1)
+        il_latent("V", chunks[2][L0], 0, VC[2])
+        widen(chunks[3][L0])
+        Q(2, K0)
+        IL(2, R0)
+        Q(2, K1)
+        IL(2, R1)
+        Q(2, R0)
+        Q(2, R1)
+        Q(2, L1)
+        clip_mul(g_st[:], rt[1][:], g_st[:])
+        Q(2, L0)
+
+        produce_b(3)
+        mm_unit(2, (0, 1, 2, 3))
+        read_unit(2)
         ck = chunks[3]
-        il(3, K0)
-        q(2, L1)
-        mm_unit(2)
-        widen(ck[L0])
-        latent_tile(ck[L0])
-        il_latent("S", ck[L0], VCOLS, U)
-        after_s(2)
-        widen(ck[L1])
-        latent_tile(ck[L1])
-        for b in range(4):
-            pe_fill(ck[L1], b)
-        il(3, K1)
-        q(3, K0)
-        il(3, R0)
-        q(3, K1)
-        il(3, R1)
-        q(3, R0)
-        il_latent("V", ck[L0], 0, VCOLS)
-        q(3, R1)
-        il(4, K0)
-        il(4, K1)
-        q(4, K0)
-        il(4, R0)
-        q(4, K1)
-        il(4, R1)
-        q(4, R0)
-        q(4, R1)
-        q(3, L0)
-        after_v(2)
-        for ps in S_HELP:
-            il(5, ps, "S", "grpH")
-        for b in range(4):
-            pe_drain(ck[L1], b)
-        nc.scalar.activation(out=fl(g_st[:]), in_=fl(g_st[:]), func=ACT.Tanh, scale=0.2)
-        q(3, L1)
-        mm_unit(3)
-        q(4, L0)
-        q(4, L1)
-        mm_unit(4)
-        after_s(3)
-        after_s(4)
-        for jj in range(2):
-            accs[(5, jj)] = bank(UNITS[5][3][jj], [P, B], F32)[:]
+        IL(3, K0)
+        IL(3, K1)
+        Q(3, K0)
+        IL(3, R0)
+        Q(3, K1)
+        IL(3, R1)
+        Q(3, R0)
+        il_latent("V", ck[L0], 0, VC[3])
+        Q(3, R1)
+        Q(3, L1)
+        Q(3, L0)
+        mm_unit(3, (0, 1))
         for ps in (K0, K1, R0, R1):
-            if ps not in S_HELP:
-                il(5, ps)
-        passes = (K0, K1, L0, L1, R0, R1)
+            IL(5, ps, "S")
+        clip_mul(rt[2][:], rt[2][:], c_t[:])
+        cbs = c_sum((4, 5, 6, 7))
+        read_unit(3)
+        th = c_tanh(cbs)
+        IL(4, K0)
+        IL(4, K1)
+        Q(4, K0)
+        IL(4, R0)
+        Q(4, K1)
+        IL(4, R1)
+        Q(4, R0)
+        Q(4, L1)
+        Q(4, R1)
+        Q(4, L0)
+        mm_unit(4, (2,))
+        o_tr(3, (0, 1))
+        read_unit(4)
+        for jj, b in enumerate((3, 4)):
+            accs[(5, jj)] = bank(b, [P, B], F32)[:]
+        passes = (L1, L0, K0, K1, R0, R1)
         for n, ps in enumerate(passes):
-            if n == 5:
-                o_stt(3)
-            q(5, ps)
+            Q(5, ps)
             for jj in range(2):
                 mx(accs[(5, jj)], 5, ps, jj, n == 0, n == 5)
-        o_tr(3)
-        o_stt(4)
-        o_tr(4)
-        r_tile(5)
-        read_gate(5, 0, "S")
-        read_gate(5, 1, "V")
-        o_stt(5)
-        o_tr(5)
-        o_out(3, work.tile([P, 2, 4 * P], F32, name="agrp", align_bytes=64)[:], "SS")
-        ost = work.tile([P, 2, 2, 2 * P], F32, name="agrp", align_bytes=64)
-        o_out(4, ost[:, 0, :, :], "SV")
-        o_out(5, ost[:, 1, :, :], "SV")
+        o_tr(4, (2,))
+        read_unit(5)
+        o_tr(5, (5,))
+        o_out(3, work.tile([P, 2, 4 * P], F32, name="agrp", align_bytes=64, bufs=3)[:], th)
+        ost = work.tile([P, 2, 2, 2 * P], F32, name="agrp", align_bytes=64, bufs=3)
+        o_out(4, ost[:, 0, :, :], th)
+        o_out(5, ost[:, 1, :, :], th)

@@ -24,9 +24,9 @@ PE_RUN = 8
 RUN = 4
 GATES = ((2 * U, "c"), (0, "i"), (U, "f"), (3 * U, "o"))
 UNITS = ((0, 0, 1024), (1, 0, 1024), (2, 0, 1024), (3, 0, 512), (3, 512, 256), (3, 768, 256))
-VC = (128, 128, 128, 128)
-PC = (256, 256, 256, 0)
-V_WIDENS = True
+VC = (128, 128, 128, 256)
+HS = (512, 512, 0)
+PC = (512, 512, 512, 0)
 K0, K1, R0, R1, L0, L1 = 0, 1, 2, 3, 4, 5
 
 
@@ -280,7 +280,7 @@ def tile_vlstmcell_kernel(tc, inputs, h_tm1, c_tm1, z_tm1, kernel, recurrent_ker
                 nc.scalar.copy(out=c_t[:, 4 * hb:4 * hb + 4, :], in_=ctp[:])
 
         def bias_turn():
-            bt = bank(2, [P, P], BF16)
+            bt = bank(0, [P, P], BF16)
             nc.tensor.transpose(bt[:], b_rows[:], ident_b[:])
             return bt
 
@@ -320,6 +320,33 @@ def tile_vlstmcell_kernel(tc, inputs, h_tm1, c_tm1, z_tm1, kernel, recurrent_ker
         def Q(u, ps):
             quantize(u, ps, grp_of(u, ps))
 
+        def help_s(u, ps):
+            gt, c0, w = UNITS[u]
+            if not HS[u]:
+                return
+            t = araw.tile([P, HS[u], PACK], BF16, name="araw", align_bytes=64)
+            interleave("S", t[:], chunks[gt][ps], c0 + w - HS[u], c0 + w)
+            grp16[(u, ps, "S")] = t
+
+        def il_rest(u, ps):
+            gt, c0, w = UNITS[u]
+            t = work.tile([P, w - HS[u], PACK], BF16, name="grpV", align_bytes=64, bufs=GV)
+            interleave("V", t[:], chunks[gt][ps], c0, c0 + w - HS[u])
+            grp16[(u, ps, "V")] = t
+            next16()
+
+        def q_part(u, ps, who):
+            gt, c0, w = UNITS[u]
+            a, b = (c0, c0 + w - HS[u]) if who == "V" else (c0 + w - HS[u], c0 + w)
+            if a == b:
+                return
+            if (gt, ps) not in codes:
+                codes[(gt, ps)] = (keep.tile([P, U], U32, name="codes", align_bytes=64),
+                                   keep.tile([P, U], U8, name="scl", align_bytes=64))
+            cd, sl = codes[(gt, ps)]
+            nc.vector.quantize_mx(out=cd[:, a:b].bitcast(FP8X4), scales=sl[:, a:b],
+                                  in_=grp16[(u, ps, who)][:].rearrange("p c t -> p (c t)"))
+
         def latent_tile(ch):
             ch["grp"] = work.tile([P, U, PACK], BF16, name="grpS", align_bytes=64)
 
@@ -335,88 +362,93 @@ def tile_vlstmcell_kernel(tc, inputs, h_tm1, c_tm1, z_tm1, kernel, recurrent_ker
             ck = chunks[gt]
             latent_tile(ck[L1])
             latent_tile(ck[L0])
-            if PC[gt]:
-                fill(ck[L0], U - PC[gt], 3)
+            for n in range(PC[gt] // 256):
+                fill(ck[L0], U - 256 * (n + 1), 3 - n)
             if gt == 0:
                 il_latent("S", ck[L0], VC[gt], U - PC[gt])
-            for b in range(4):
-                drain(ck[L1], 256 * b)
-            if PC[gt]:
-                drain(ck[L0], U - PC[gt])
+            else:
+                for b in range(4):
+                    drain(ck[L1], 256 * b)
+            for n in range(PC[gt] // 256):
+                drain(ck[L0], U - 256 * (n + 1))
             if gt > 0:
                 il_latent("S", ck[L0], VC[gt], U - PC[gt])
 
         ck = chunks[0]
         nc.sync.dma_start(out=sc[:], in_=recurrent_latent_scale.rearrange("(g p t) o -> p g (t o)", g=2, p=P, t=PACK))
-        first16 = load(order16[0], pieces=4)
         l0p = load(order8[0], planes=True)
         l1p = load(order8[1], planes=True)
-        st["n16"], st["n8"] = 1, 2
+        st["n8"] = 2
         for n in range(4):
-            dma([l0p[n], l1p[n], first16[n]])
+            dma([l0p[n], l1p[n]])
         next16()
         next8()
         next16()
         wide_tile(ck[L0])
         wide_tile(ck[L1])
-        il(0, K0)
         for n in range(4):
             widen_plane(ck[L0], n, "S")
-            widen_plane(ck[L1], n, "V" if V_WIDENS else "S")
-            il_go(0, K0, "V", (256 * n, 256 * n + 256))
+            widen_plane(ck[L1], n, "V")
         next8()
+        next16()
         next16()
         act_load(inputs)
         act_load(h_tm1)
         next16()
         act_load(z_tm1)
-        act_load(c_tm1)
         nc.sync.dma_start(out=b_rows[0:32, :], in_=bias.rearrange("(r c) -> r c", c=P))
         next8()
-        fill_l1(0)
         produce_b(0)
+        il_latent("V", ck[L1], 0, U)
+        IL(0, K0)
         il_latent("V", ck[L0], 0, VC[0])
-        Q(0, K0)
+        Q(0, L1)
         IL(0, K1)
+        Q(0, K0)
         IL(0, R0)
         Q(0, K1)
-        IL(0, R1)
-        Q(0, R0)
-        Q(0, L1)
-        Q(0, R1)
-        Q(0, L0)
-
         widen(chunks[1][L1])
         fill_l1(1)
         widen(chunks[1][L0])
+        help_s(0, R1)
+        il_rest(0, R1)
+        Q(0, R0)
+        Q(0, L0)
+        q_part(0, R1, "V")
+        q_part(0, R1, "S")
+
         for s in range(3):
             act_turn(s)
-        c_turn()
         bt = bias_turn()
         produce_b(1)
         il_latent("V", chunks[1][L0], 0, VC[1])
         widen(chunks[2][L1])
+        help_s(1, R1)
         IL(1, K0)
+        act_load(c_tm1)
         act_q(0)
         act_q(1)
-        IL(1, K1)
-        Q(1, K0)
         act_q(2)
         bias_out(bt)
         mm_unit(0, (0, 1, 2, 3))
         fill_l1(2)
         read_unit(0)
         widen(chunks[2][L0])
+        c_turn()
+        IL(1, K1)
+        Q(1, K0)
         IL(1, R0)
         Q(1, K1)
-        IL(1, R1)
+        il_rest(1, R1)
         Q(1, R0)
-        Q(1, R1)
+        q_part(1, R1, "V")
+        q_part(1, R1, "S")
         Q(1, L1)
         Q(1, L0)
 
         produce_b(2)
         widen(chunks[3][L1])
+        help_s(2, R1)
         mm_unit(1, (0, 1, 2, 3))
         fill_l1(3)
         read_unit(1)
@@ -427,58 +459,66 @@ def tile_vlstmcell_kernel(tc, inputs, h_tm1, c_tm1, z_tm1, kernel, recurrent_ker
         Q(2, K0)
         IL(2, R0)
         Q(2, K1)
-        IL(2, R1)
+        il_rest(2, R1)
         Q(2, R0)
-        Q(2, R1)
+        q_part(2, R1, "V")
+        q_part(2, R1, "S")
         Q(2, L1)
-        clip_mul(g_st[:], rt[1][:], g_st[:])
         Q(2, L0)
+        clip_mul(g_st[:], rt[1][:], g_st[:])
 
         produce_b(3)
         mm_unit(2, (0, 1, 2, 3))
         read_unit(2)
         ck = chunks[3]
+
+        def open_unit(u, bks):
+            for jj, b in enumerate(bks):
+                accs[(u, jj)] = bank(b, [P, B], F32)[:]
+
+        def QM(u, ps, first=False, last=False):
+            Q(u, ps)
+            for jj in range(UNITS[u][2] // P):
+                mx(accs[(u, jj)], u, ps, jj, first, last)
+
+        open_unit(3, (4, 5, 6, 7))
         IL(3, K0)
         IL(3, K1)
-        Q(3, K0)
+        QM(3, K0, first=True)
         IL(3, R0)
-        Q(3, K1)
+        QM(3, K1)
         IL(3, R1)
-        Q(3, R0)
+        QM(3, R0)
         il_latent("V", ck[L0], 0, VC[3])
-        Q(3, R1)
-        Q(3, L1)
-        Q(3, L0)
-        mm_unit(3, (0, 1))
+        QM(3, R1)
+        QM(3, L1)
+        QM(3, L0, last=True)
         for ps in (K0, K1, R0, R1):
             IL(5, ps, "S")
         clip_mul(rt[2][:], rt[2][:], c_t[:])
-        cbs = c_sum((4, 5, 6, 7))
+        cbs = c_sum((0, 1, 2, 3))
         read_unit(3)
         th = c_tanh(cbs)
+        open_unit(4, (4, 5))
         IL(4, K0)
         IL(4, K1)
-        Q(4, K0)
+        QM(4, K0, first=True)
         IL(4, R0)
-        Q(4, K1)
+        QM(4, K1)
         IL(4, R1)
-        Q(4, R0)
-        Q(4, L1)
-        Q(4, R1)
-        Q(4, L0)
-        mm_unit(4, (2,))
+        QM(4, R0)
+        QM(4, L1)
+        QM(4, R1)
         o_tr(3, (0, 1))
+        QM(4, L0, last=True)
         read_unit(4)
-        for jj, b in enumerate((3, 4)):
-            accs[(5, jj)] = bank(b, [P, B], F32)[:]
+        open_unit(5, (6, 7))
         passes = (L1, L0, K0, K1, R0, R1)
         for n, ps in enumerate(passes):
-            Q(5, ps)
-            for jj in range(2):
-                mx(accs[(5, jj)], 5, ps, jj, n == 0, n == 5)
+            QM(5, ps, n == 0, n == 5)
         o_tr(4, (2,))
         read_unit(5)
-        o_tr(5, (5,))
+        o_tr(5, (3,))
         o_out(3, work.tile([P, 2, 4 * P], F32, name="agrp", align_bytes=64, bufs=3)[:], th)
         ost = work.tile([P, 2, 2, 2 * P], F32, name="agrp", align_bytes=64, bufs=3)
         o_out(4, ost[:, 0, :, :], th)

@@ -196,19 +196,23 @@ def tile_vlstmcell_kernel(tc, inputs, h_tm1, c_tm1, z_tm1, kernel, recurrent_ker
             for jj in range(nt):
                 read_gate(u, jj)
 
-        def c_sum(bks):
+        def c_sum_a(bks):
             cbs = []
             for a in range(2):
                 for h in range(2):
                     cb = bank(bks[2 * a + h], [P, 4, P], F32)
                     for jj in range(4):
-                        j = 4 * h + jj
-                        nc.tensor.matmul(out=cb[:, jj, :], lhsT=g_st[:, j, P * a:P * a + P], rhs=ident_f[:], is_transpose=True,
-                                         start=True, stop=False)
-                        nc.tensor.matmul(out=cb[:, jj, :], lhsT=rt[2][:, j, P * a:P * a + P], rhs=ident_f[:], is_transpose=True,
-                                         start=False, stop=True)
+                        nc.tensor.matmul(out=cb[:, jj, :], lhsT=g_st[:, 4 * h + jj, P * a:P * a + P], rhs=ident_f[:], is_transpose=True,
+                                         start=(jj == 0), stop=False)
                     cbs.append(cb)
             return cbs
+
+        def c_sum_b(cbs):
+            for a in range(2):
+                for h in range(2):
+                    for jj in range(4):
+                        nc.tensor.matmul(out=cbs[2 * a + h][:, jj, :], lhsT=rt[2][:, 4 * h + jj, P * a:P * a + P], rhs=ident_f[:],
+                                         is_transpose=True, start=False, stop=(jj == 3))
 
         def c_tanh(cbs):
             th = work.tile([P, 2, U], F32, name="r8", bufs=1)
@@ -258,7 +262,7 @@ def tile_vlstmcell_kernel(tc, inputs, h_tm1, c_tm1, z_tm1, kernel, recurrent_ker
             words = acts[s][:].bitcast(F32)
             agrp = work.tile([P, 2, B, PACK], BF16, name="agrp", align_bytes=64, bufs=3)
             for g in range(2):
-                xt = bank((2 * s + g) % 3, [P, 2, B], F32)
+                xt = bank((2 * s + g) % 4, [P, 2, B], F32)
                 for a in range(2):
                     for u2 in range(2):
                         nc.tensor.transpose(xt[:, u2, P * a:P * a + P], words[:, a, 256 * g + u2:256 * (g + 1):2], ident_f[:])
@@ -400,8 +404,8 @@ def tile_vlstmcell_kernel(tc, inputs, h_tm1, c_tm1, z_tm1, kernel, recurrent_ker
         next8()
         produce_b(0)
         il_latent("V", ck[L1], 0, U)
-        IL(0, K0)
         il_latent("V", ck[L0], 0, VC[0])
+        IL(0, K0)
         Q(0, L1)
         IL(0, K1)
         Q(0, K0)
@@ -452,23 +456,39 @@ def tile_vlstmcell_kernel(tc, inputs, h_tm1, c_tm1, z_tm1, kernel, recurrent_ker
         mm_unit(1, (0, 1, 2, 3))
         fill_l1(3)
         read_unit(1)
+        fb = [bank(b, [P, 2, B], F32) for b in range(4)]
+        for jj in range(8):
+            accs[(2, jj)] = fb[jj % 4][:, jj // 4, :]
+
+        def first_half(ps, first=False, last=False):
+            for jj in range(4):
+                mx(accs[(2, jj)], 2, ps, jj, first, last)
+
         IL(2, K0)
         IL(2, K1)
         il_latent("V", chunks[2][L0], 0, VC[2])
         widen(chunks[3][L0])
         Q(2, K0)
+        first_half(K0, first=True)
         IL(2, R0)
         Q(2, K1)
+        first_half(K1)
         il_rest(2, R1)
         Q(2, R0)
+        first_half(R0)
         q_part(2, R1, "V")
         q_part(2, R1, "S")
+        first_half(R1)
         Q(2, L1)
+        first_half(L1)
         Q(2, L0)
+        first_half(L0, last=True)
         clip_mul(g_st[:], rt[1][:], g_st[:])
 
         produce_b(3)
-        mm_unit(2, (0, 1, 2, 3))
+        for jj in range(4, 8):
+            for ps in range(6):
+                mx(accs[(2, jj)], 2, ps, jj, ps == 0, ps == 5)
         read_unit(2)
         ck = chunks[3]
 
@@ -495,8 +515,9 @@ def tile_vlstmcell_kernel(tc, inputs, h_tm1, c_tm1, z_tm1, kernel, recurrent_ker
         QM(3, L0, last=True)
         for ps in (K0, K1, R0, R1):
             IL(5, ps, "S")
+        cbs = c_sum_a((0, 1, 2, 3))
         clip_mul(rt[2][:], rt[2][:], c_t[:])
-        cbs = c_sum((0, 1, 2, 3))
+        c_sum_b(cbs)
         read_unit(3)
         th = c_tanh(cbs)
         open_unit(4, (4, 5))

@@ -161,12 +161,14 @@ def tile_vlstmcell_kernel(tc, inputs, h_tm1, c_tm1, z_tm1, kernel, recurrent_ker
         accs = {}
 
         def mm_unit(u, banks):
-            for jj in range(UNITS[u][2] // P):
-                if jj % 2 == 0:
-                    bk = bank(banks[jj // 2], [P, 2, B], F32)
-                accs[(u, jj)] = bk[:, jj % 2, :]
-                for ps in range(6):
-                    mx(accs[(u, jj)], u, ps, jj, ps == 0, ps == 5)
+            for pair in range(2):
+                bks = [bank(banks[2 * pair + n], [P, 2, B], F32) for n in range(2)]
+                for half in range(2):
+                    for ps in range(6):
+                        for n in range(2):
+                            jj = 4 * pair + 2 * n + half
+                            accs[(u, jj)] = bks[n][:, half, :]
+                            mx(accs[(u, jj)], u, ps, jj, ps == 0, ps == 5)
 
         rt = {}
 
@@ -486,9 +488,10 @@ def tile_vlstmcell_kernel(tc, inputs, h_tm1, c_tm1, z_tm1, kernel, recurrent_ker
         clip_mul(g_st[:], rt[1][:], g_st[:])
 
         produce_b(3)
-        for jj in range(4, 8):
+        for pair in range(2):
             for ps in range(6):
-                mx(accs[(2, jj)], 2, ps, jj, ps == 0, ps == 5)
+                for jj in (4 + 2 * pair, 5 + 2 * pair):
+                    mx(accs[(2, jj)], 2, ps, jj, ps == 0, ps == 5)
         read_unit(2)
         ck = chunks[3]
 

@@ -375,10 +375,10 @@ def tile_vlstmcell_kernel(tc, inputs, h_tm1, c_tm1, z_tm1, kernel, recurrent_ker
             else:
                 for b in range(4):
                     drain(ck[L1], 256 * b)
-            for n in range(PC[gt] // 256):
-                drain(ck[L0], U - 256 * (n + 1))
             if gt > 0:
                 il_latent("S", ck[L0], VC[gt], U - PC[gt])
+                for n in range(PC[gt] // 256):
+                    drain(ck[L0], U - 256 * (n + 1))
 
         ck = chunks[0]
         nc.sync.dma_start(out=sc[:], in_=recurrent_latent_scale.rearrange("(g p t) o -> p g (t o)", g=2, p=P, t=PACK))
@@ -390,8 +390,8 @@ def tile_vlstmcell_kernel(tc, inputs, h_tm1, c_tm1, z_tm1, kernel, recurrent_ker
         next16()
         next8()
         next16()
-        wide_tile(ck[L0])
         wide_tile(ck[L1])
+        wide_tile(ck[L0])
         for n in range(4):
             widen_plane(ck[L0], n, "S")
             widen_plane(ck[L1], n, "V")
@@ -400,8 +400,8 @@ def tile_vlstmcell_kernel(tc, inputs, h_tm1, c_tm1, z_tm1, kernel, recurrent_ker
         next16()
         act_load(inputs)
         act_load(h_tm1)
-        next16()
         act_load(z_tm1)
+        next16()
         nc.sync.dma_start(out=b_rows[0:32, :], in_=bias.rearrange("(r c) -> r c", c=P))
         next8()
         produce_b(0)
@@ -415,6 +415,8 @@ def tile_vlstmcell_kernel(tc, inputs, h_tm1, c_tm1, z_tm1, kernel, recurrent_ker
         Q(0, K1)
         widen(chunks[1][L1])
         fill_l1(1)
+        for n in range(PC[0] // 256):
+            drain(ck[L0], U - 256 * (n + 1))
         widen(chunks[1][L0])
         help_s(0, R1)
         il_rest(0, R1)

@@ -385,8 +385,8 @@ def tile_vlstmcell_kernel(tc, inputs, h_tm1, c_tm1, z_tm1, kernel, recurrent_ker
         l0p = load(order8[0], planes=True)
         l1p = load(order8[1], planes=True)
         st["n8"] = 2
-        for n in range(4):
-            dma([l0p[n], l1p[n]])
+        for pl in (l0p[0], l1p[0], l1p[1], l0p[1], l1p[2], l1p[3], l0p[2], l0p[3]):
+            dma([pl])
         next16()
         next8()
         next16()
@@ -430,10 +430,10 @@ def tile_vlstmcell_kernel(tc, inputs, h_tm1, c_tm1, z_tm1, kernel, recurrent_ker
         bt = bias_turn()
         produce_b(1)
         il_latent("V", chunks[1][L0], 0, VC[1])
+        act_load(c_tm1)
         widen(chunks[2][L1])
         help_s(1, R1)
         IL(1, K0)
-        act_load(c_tm1)
         act_q(0)
         act_q(1)
         act_q(2)

from contextlib import ExitStack

import concourse.masks as masks
import concourse.mybir as mybir

B, I, U = 256, 1024, 1024
FLOPS = 2 * B * (I + U + U) * 4 * U

F32 = mybir.dt.float32
BF16 = mybir.dt.bfloat16
U32 = mybir.dt.uint32
U8 = mybir.dt.uint8
FP8 = mybir.dt.float8_e4m3fn
FP8X4 = mybir.dt.float8_e4m3fn_x4
ACT = mybir.ActivationFunctionType
ALU = mybir.AluOpType

P = 128
PACK = 4
D16 = 5
D8 = 3
GV = 3
PE_RUN = 8
RUN = 4
GATES = ((2 * U, "c"), (0, "i"), (U, "f"), (3 * U, "o"))
UNITS = ((0, 0, 1024), (1, 0, 1024), (2, 0, 1024), (3, 0, 512), (3, 512, 256), (3, 768, 256))
VC = (128, 128, 128, 256)
HS = (512, 512, 0)
PC = (512, 512, 512, 0)
K0, K1, R0, R1, L0, L1 = 0, 1, 2, 3, 4, 5


def tile_vlstmcell_kernel(tc, inputs, h_tm1, c_tm1, z_tm1, kernel, recurrent_kernel,
                                      recurrent_latent_bytes, recurrent_latent_scale, bias, out):
    nc = tc.nc
    with ExitStack() as ctx:
        const = ctx.enter_context(tc.tile_pool(name="const", bufs=1))
        raw16 = ctx.enter_context(tc.tile_pool(name="raw16", bufs=D16))
        raw8 = ctx.enter_context(tc.tile_pool(name="raw8", bufs=D8))
        work = ctx.enter_context(tc.tile_pool(name="work", bufs=2))
        keep = ctx.enter_context(tc.tile_pool(name="keep", bufs=12))
        araw = ctx.enter_context(tc.tile_pool(name="araw", bufs=4))
        psum = ctx.enter_context(tc.psum_pool(name="psum", bufs=1))
        ctx.enter_context(tc.manual_schedule())

        def bank(i, shape, dtype):
            return psum.tile(shape, dtype, name="bank%d" % i, tag="bank%d" % i)

        w_views = [w.rearrange("(g p t) n -> g p t n", g=2, p=P, t=PACK)
                   for w in (kernel, recurrent_kernel, recurrent_latent_bytes)]
        chunks = [[{"ps": ps, "col": GATES[gt][0]} for ps in range(6)] for gt in range(4)]
        order16 = [chunks[gt][ps] for gt in range(4) for ps in (K0, K1, R0, R1)]
        order8 = [chunks[0][L0], chunks[0][L1]] + [chunks[gt][ps] for gt in range(1, 4) for ps in (L1, L0)]
        st = {"n16": 0, "n8": 0}

        ident_f = const.tile([P, P], F32, name="ident_f")
        ident_b = const.tile([P, P], BF16, name="ident_b")
        b_rows = const.tile([P, P], BF16, name="b_rows")
        warm = const.tile([P, 1], F32, name="warm")
        sc = const.tile([P, 2, PACK], F32, name="sc")
        bias_pl = const.tile([P, 32], F32, name="bias_pl")
        bias_hs = const.tile([P, 32], F32, name="bias_hs")
        a_codes = const.tile([P, 6, B], U32, name="a_codes", align_bytes=64)
        a_scl = const.tile([P, 6, B], U8, name="a_scl", align_bytes=64)
        g_st = const.tile([P, 8, B], F32, name="g_st")
        c_t = const.tile([P, 8, B], BF16, name="c_t")
        nc.gpsimd.memset(warm[:], 0.0)
        nc.scalar.activation(out=warm[:], in_=warm[:], func=ACT.Tanh)
        masks.make_identity(nc, ident_b[:])
        masks.make_identity(nc, ident_f[:])
        nc.gpsimd.memset(b_rows[:], 0.0)

        def load(ch, pieces=1, planes=False):
            s, g = divmod(ch["ps"], 2)
            col = ch["col"]
            if s == 2:
                raw = raw8.tile([P, PACK, U], U8, name="raw8")
            else:
                raw = raw16.tile([P, PACK, U], BF16, name="raw16")
            ch["raw"] = raw
            ch["src"] = raw
            todo = []
            if planes:
                for t in range(PACK):
                    todo.append((raw[:, t, :], w_views[s][g][:, t, col:col + U]))
            else:
                step = U // pieces
                for a in range(0, U, step):
                    todo.append((raw[:, :, a:a + step], w_views[s][g][:, :, col + a:col + a + step]))
            return todo

        def dma(pairs):
            for o, i in pairs:
                nc.sync.dma_start(out=o, in_=i)

        def next16():
            if st["n16"] < len(order16):
                dma(load(order16[st["n16"]]))
                st["n16"] += 1

        def next8():
            if st["n8"] < len(order8):
                dma(load(order8[st["n8"]]))
                st["n8"] += 1

        def wide_tile(ch):
            ch["src"] = work.tile([P, PACK, U], BF16, name="wide")

        def widen_plane(ch, t, eng):
            g = ch["ps"] % 2
            if eng == "S":
                nc.scalar.activation(out=ch["src"][:, t, :], in_=ch["raw"][:, t, :].bitcast(FP8), func=ACT.Copy,
                                     scale=sc[:, g, t:t + 1])
            else:
                nc.vector.tensor_scalar(out=ch["src"][:, t, :], in0=ch["raw"][:, t, :].bitcast(FP8), scalar1=sc[:, g, t:t + 1],
                                        scalar2=None, op0=ALU.mult)

        def widen(ch):
            wide_tile(ch)
            for t in range(PACK):
                widen_plane(ch, t, "S")
            next8()

        def interleave(eng, grp, ch, c0, c1):
            o = grp.rearrange("p (c i) t -> p c t i", i=RUN)
            i = ch["src"][:, :, c0:c1].rearrange("p t (c i) -> p c t i", i=RUN)
            if eng == "V":
                nc.vector.tensor_copy(out=o, in_=i)
            else:
                nc.scalar.copy(out=o, in_=i)

        def fill(ch, c0, b):
            pb = bank(b, [P, 256, PACK], BF16)
            for h in range(2):
                c = c0 + 128 * h
                nc.tensor.matmul(out=pb[:, 128 * h:128 * h + 128, :].rearrange("p (c i) t -> p c t i", i=PE_RUN), lhsT=ident_b[:],
                                 rhs=ch["src"][:, :, c:c + 128].rearrange("p t (c i) -> p c t i", i=PE_RUN),
                                 start=True, stop=True)
            ch["pb%d" % c0] = pb

        def drain(ch, c0):
            nc.scalar.copy(out=ch["grp"][:, c0:c0 + 256, :], in_=ch["pb%d" % c0][:])

        codes = {}

        def quantize(u, ps, grp):
            gt, c0, w = UNITS[u]
            if (gt, ps) not in codes:
                codes[(gt, ps)] = (keep.tile([P, U], U32, name="codes", align_bytes=64),
                                   keep.tile([P, U], U8, name="scl", align_bytes=64))
            cd, sl = codes[(gt, ps)]
            nc.vector.quantize_mx(out=cd[:, c0:c0 + w].bitcast(FP8X4), scales=sl[:, c0:c0 + w],
                                  in_=grp.rearrange("p c t -> p (c t)"))

        def mx(acc, u, ps, jj, start, stop):
            cd, sl = codes[(UNITS[u][0], ps)]
            c = UNITS[u][1] + P * jj
            nc.tensor.matmul_mx(out=acc, lhsT=cd[:, c:c + P].bitcast(FP8X4), lhsT_scale=sl[:, c:c + P],
                                rhs=a_codes[:, ps, :].bitcast(FP8X4), rhs_scale=a_scl[:, ps, :], start=start, stop=stop)

        accs = {}

        def mm_unit(u, banks):
            for pair in range(2):
                bks = [bank(banks[2 * pair + n], [P, 2, B], F32) for n in range(2)]
                for half in range(2):
                    for ps in range(6):
                        for n in range(2):
                            jj = 4 * pair + 2 * n + half
                            accs[(u, jj)] = bks[n][:, half, :]
                            mx(accs[(u, jj)], u, ps, jj, ps == 0, ps == 5)

        rt = {}

        def kind(u):
            return GATES[UNITS[u][0]][1]

        def read_gate(u, jj):
            j = UNITS[u][1] // P + jj
            col = GATES[UNITS[u][0]][0] // P + j
            if kind(u) == "c":
                nc.scalar.activation(out=g_st[:, j, :], in_=accs[(u, jj)], func=ACT.Tanh,
                                     bias=bias_pl[:, col:col + 1], scale=1.0)
            else:
                nc.scalar.activation(out=rt[u][:, jj, :], in_=accs[(u, jj)], func=ACT.Relu,
                                     bias=bias_hs[:, col:col + 1], scale=0.2)

        def fl(ap):
            return ap.rearrange("p j b -> p (j b)")

        def clip_mul(o, r, other):
            nc.vector.scalar_tensor_tensor(out=fl(o), in0=fl(r), scalar=1.0, in1=fl(other), op0=ALU.min, op1=ALU.mult)

        def read_unit(u):
            nt = UNITS[u][2] // P
            if kind(u) != "c":
                rt[u] = work.tile([P, nt, B], F32, name="r%d" % nt, bufs=(2 if nt == 2 else 1))
            for jj in range(nt):
                read_gate(u, jj)

        def c_sum_a(bks):
            cbs = []
            for a in range(2):
                for h in range(2):
                    cb = bank(bks[2 * a + h], [P, 4, P], F32)
                    for jj in range(4):
                        nc.tensor.matmul(out=cb[:, jj, :], lhsT=g_st[:, 4 * h + jj, P * a:P * a + P], rhs=ident_f[:], is_transpose=True,
                                         start=(jj == 0), stop=False)
                    cbs.append(cb)
            return cbs

        def c_sum_b(cbs):
            for a in range(2):
                for h in range(2):
                    for jj in range(4):
                        nc.tensor.matmul(out=cbs[2 * a + h][:, jj, :], lhsT=rt[2][:, 4 * h + jj, P * a:P * a + P], rhs=ident_f[:],
                                         is_transpose=True, start=False, stop=(jj == 3))

        def c_tanh(cbs):
            th = work.tile([P, 2, U], F32, name="r8", bufs=1)
            for a in range(2):
                for h in range(2):
                    nc.scalar.activation(out=th[:, a, 512 * h:512 * h + 512], in_=cbs[2 * a + h][:].rearrange("p j n -> p (j n)"),
                                         func=ACT.Tanh)
            return th

        tps = {}

        def o_tr(u, bks):
            nt = UNITS[u][2] // P
            for a in range(2):
                if len(bks) == 2:
                    tp = bank(bks[a], [P, nt * P], F32)[:]
                else:
                    if a == 0:
                        both = bank(bks[0], [P, 2, nt * P], F32)
                    tp = both[:, a, :]
                for jj in range(nt):
                    nc.tensor.transpose(tp[:, P * jj:P * jj + P], rt[u][:, jj, P * a:P * a + P], ident_f[:])
                tps[(u, a)] = tp
            if len(bks) == 1:
                tps[u] = both

        def o_out(u, ost, th):
            c0, w = UNITS[u][1], UNITS[u][2]
            if u in tps:
                nc.vector.scalar_tensor_tensor(out=ost, in0=tps[u][:], scalar=1.0, in1=th[:, :, c0:c0 + w], op0=ALU.min, op1=ALU.mult)
            else:
                for a in range(2):
                    nc.vector.scalar_tensor_tensor(out=ost[:, a, :], in0=tps[(u, a)], scalar=1.0, in1=th[:, a, c0:c0 + w],
                                                   op0=ALU.min, op1=ALU.mult)
            nc.sync.dma_start(out=out.rearrange("(a p) n -> p a n", a=2)[:, :, c0:c0 + w], in_=ost)

        acts = []

        def act_load(x):
            xa = araw.tile([P, 2, I], BF16, name="araw", align_bytes=64)
            nc.sync.dma_start(out=xa[:], in_=x.rearrange("(a p) k -> p a k", a=2))
            acts.append(xa)

        agrps = {}

        def act_turn(s):
            words = acts[s][:].bitcast(F32)
            agrp = work.tile([P, 2, B, PACK], BF16, name="agrp", align_bytes=64, bufs=3)
            for g in range(2):
                xt = bank((2 * s + g) % 4, [P, 2, B], F32)
                for a in range(2):
                    for u2 in range(2):
                        nc.tensor.transpose(xt[:, u2, P * a:P * a + P], words[:, a, 256 * g + u2:256 * (g + 1):2], ident_f[:])
                nc.scalar.copy(out=agrp[:, g, :, :].bitcast(F32), in_=xt[:].rearrange("p u r -> p r u"))
            agrps[s] = agrp

        def act_q(s):
            nc.vector.quantize_mx(out=a_codes[:, 2 * s:2 * s + 2, :].rearrange("p g r -> p (g r)").bitcast(FP8X4),
                                  scales=a_scl[:, 2 * s:2 * s + 2, :].rearrange("p g r -> p (g r)"),
                                  in_=agrps[s][:].rearrange("p g r t -> p (g r t)"))

        def c_turn():
            for hb in range(2):
                ctp = bank(hb, [P, 4, B], BF16)
                for jj in range(4):
                    for a in range(2):
                        j = 4 * hb + jj
                        nc.tensor.transpose(ctp[:, jj, P * a:P * a + P], acts[3][:, a, P * j:P * j + P], ident_b[:])
                nc.scalar.copy(out=c_t[:, 4 * hb:4 * hb + 4, :], in_=ctp[:])

        def bias_turn():
            bt = bank(0, [P, P], BF16)
            nc.tensor.transpose(bt[:], b_rows[:], ident_b[:])
            return bt

        def bias_out(bt):
            nc.vector.tensor_copy(out=bias_pl[:], in_=bt[:, 0:32])
            nc.vector.tensor_scalar(out=bias_hs[:], in0=bt[:, 0:32], scalar1=0.2, scalar2=0.5, op0=ALU.mult, op1=ALU.add)

        grp16 = {}

        def grp_of(u, ps):
            c0, w = UNITS[u][1], UNITS[u][2]
            if ps in (L0, L1):
                return chunks[UNITS[u][0]][ps]["grp"][:, c0:c0 + w, :]
            return grp16[(u, ps)][:]

        def il(u, ps, eng="V", pieces=1):
            gt, c0, w = UNITS[u]
            if eng == "V":
                t = work.tile([P, w, PACK], BF16, name="grpV", align_bytes=64, bufs=GV)
            else:
                t = araw.tile([P, w, PACK], BF16, name="araw", align_bytes=64)
            grp16[(u, ps)] = t
            return t

        def il_go(u, ps, eng="V", part=None):
            gt, c0, w = UNITS[u]
            t = grp16[(u, ps)]
            a, b = part or (0, w)
            interleave(eng, t[:, a:b, :], chunks[gt][ps], c0 + a, c0 + b)
            if c0 + b == U:
                next16()

        def IL(u, ps, eng="V"):
            il(u, ps, eng)
            il_go(u, ps, eng)

        def Q(u, ps):
            quantize(u, ps, grp_of(u, ps))

        def help_s(u, ps):
            gt, c0, w = UNITS[u]
            if not HS[u]:
                return
            t = araw.tile([P, HS[u], PACK], BF16, name="araw", align_bytes=64)
            interleave("S", t[:], chunks[gt][ps], c0 + w - HS[u], c0 + w)
            grp16[(u, ps, "S")] = t

        def il_rest(u, ps):
            gt, c0, w = UNITS[u]
            t = work.tile([P, w - HS[u], PACK], BF16, name="grpV", align_bytes=64, bufs=GV)
            interleave("V", t[:], chunks[gt][ps], c0, c0 + w - HS[u])
            grp16[(u, ps, "V")] = t
            next16()

        def q_part(u, ps, who):
            gt, c0, w = UNITS[u]
            a, b = (c0, c0 + w - HS[u]) if who == "V" else (c0 + w - HS[u], c0 + w)
            if a == b:
                return
            if (gt, ps) not in codes:
                codes[(gt, ps)] = (keep.tile([P, U], U32, name="codes", align_bytes=64),
                                   keep.tile([P, U], U8, name="scl", align_bytes=64))
            cd, sl = codes[(gt, ps)]
            nc.vector.quantize_mx(out=cd[:, a:b].bitcast(FP8X4), scales=sl[:, a:b],
                                  in_=grp16[(u, ps, who)][:].rearrange("p c t -> p (c t)"))

        def latent_tile(ch):
            ch["grp"] = work.tile([P, U, PACK], BF16, name="grpS", align_bytes=64)

        def il_latent(eng, ch, c0, c1):
            if c1 > c0:
                interleave(eng, ch["grp"][:, c0:c1, :], ch, c0, c1)

        def fill_l1(gt):
            for b in range(4):
                fill(chunks[gt][L1], 256 * b, 4 + b)

        def produce_b(gt):
            ck = chunks[gt]
            latent_tile(ck[L1])
            latent_tile(ck[L0])
            for n in range(PC[gt] // 256):
                fill(ck[L0], U - 256 * (n + 1), 3 - n)
            if gt == 0:
                il_latent("S", ck[L0], VC[gt], U - PC[gt])
            else:
                for b in range(4):
                    drain(ck[L1], 256 * b)
            if gt > 0:
                il_latent("S", ck[L0], VC[gt], U - PC[gt])
                for n in range(PC[gt] // 256):
                    drain(ck[L0], U - 256 * (n + 1))

        ck = chunks[0]
        nc.sync.dma_start(out=sc[:], in_=recurrent_latent_scale.rearrange("(g p t) o -> p g (t o)", g=2, p=P, t=PACK))
        l0p = load(order8[0], planes=True)
        l1p = load(order8[1], planes=True)
        st["n8"] = 2
        for pl in (l0p[0], l1p[0], l1p[1], l0p[1], l1p[2], l1p[3], l0p[2], l0p[3]):
            dma([pl])
        next16()
        next8()
        next16()
        wide_tile(ck[L1])
        wide_tile(ck[L0])
        for n in range(4):
            widen_plane(ck[L0], n, "S")
            widen_plane(ck[L1], n, "V")
        next8()
        next16()
        next16()
        act_load(inputs)
        act_load(h_tm1)
        act_load(z_tm1)
        next16()
        nc.sync.dma_start(out=b_rows[0:32, :], in_=bias.rearrange("(r c) -> r c", c=P))
        next8()
        produce_b(0)
        il_latent("V", ck[L1], 0, U)
        il_latent("V", ck[L0], 0, VC[0])
        IL(0, K0)
        Q(0, L1)
        IL(0, K1)
        Q(0, K0)
        IL(0, R0)
        Q(0, K1)
        widen(chunks[1][L1])
        fill_l1(1)
        for n in range(PC[0] // 256):
            drain(ck[L0], U - 256 * (n + 1))
        widen(chunks[1][L0])
        help_s(0, R1)
        il_rest(0, R1)
        Q(0, R0)
        Q(0, L0)
        q_part(0, R1, "V")
        q_part(0, R1, "S")

        for s in range(3):
            act_turn(s)
        bt = bias_turn()
        produce_b(1)
        il_latent("V", chunks[1][L0], 0, VC[1])
        act_load(c_tm1)
        widen(chunks[2][L1])
        help_s(1, R1)
        IL(1, K0)
        act_q(0)
        act_q(1)
        act_q(2)
        bias_out(bt)
        mm_unit(0, (0, 1, 2, 3))
        fill_l1(2)
        read_unit(0)
        widen(chunks[2][L0])
        c_turn()
        IL(1, K1)
        Q(1, K0)
        IL(1, R0)
        Q(1, K1)
        il_rest(1, R1)
        Q(1, R0)
        q_part(1, R1, "V")
        q_part(1, R1, "S")
        Q(1, L1)
        Q(1, L0)

        produce_b(2)
        widen(chunks[3][L1])
        help_s(2, R1)
        mm_unit(1, (0, 1, 2, 3))
        fill_l1(3)
        read_unit(1)
        fb = [bank(b, [P, 2, B], F32) for b in range(4)]
        for jj in range(8):
            accs[(2, jj)] = fb[jj % 4][:, jj // 4, :]

        def first_half(ps, first=False, last=False):
            for jj in range(4):
                mx(accs[(2, jj)], 2, ps, jj, first, last)

        IL(2, K0)
        IL(2, K1)
        il_latent("V", chunks[2][L0], 0, VC[2])
        widen(chunks[3][L0])
        Q(2, K0)
        first_half(K0, first=True)
        IL(2, R0)
        Q(2, K1)
        first_half(K1)
        il_rest(2, R1)
        Q(2, R0)
        first_half(R0)
        q_part(2, R1, "V")
        q_part(2, R1, "S")
        first_half(R1)
        Q(2, L1)
        first_half(L1)
        Q(2, L0)
        first_half(L0, last=True)
        clip_mul(g_st[:], rt[1][:], g_st[:])

        produce_b(3)
        for pair in range(2):
            for ps in range(6):
                for jj in (4 + 2 * pair, 5 + 2 * pair):
                    mx(accs[(2, jj)], 2, ps, jj, ps == 0, ps == 5)
        read_unit(2)
        ck = chunks[3]

        def open_unit(u, bks):
            for jj, b in enumerate(bks):
                accs[(u, jj)] = bank(b, [P, B], F32)[:]

        def QM(u, ps, first=False, last=False):
            Q(u, ps)
            for jj in range(UNITS[u][2] // P):
                mx(accs[(u, jj)], u, ps, jj, first, last)

        open_unit(3, (4, 5, 6, 7))
        IL(3, K0)
        IL(3, K1)
        QM(3, K0, first=True)
        IL(3, R0)
        QM(3, K1)
        IL(3, R1)
        QM(3, R0)
        il_latent("V", ck[L0], 0, VC[3])
        QM(3, R1)
        QM(3, L1)
        QM(3, L0, last=True)
        for ps in (K0, K1, R0, R1):
            IL(5, ps, "S")
        cbs = c_sum_a((0, 1, 2, 3))
        clip_mul(rt[2][:], rt[2][:], c_t[:])
        c_sum_b(cbs)
        read_unit(3)
        th = c_tanh(cbs)
        open_unit(4, (4, 5))
        IL(4, K0)
        IL(4, K1)
        QM(4, K0, first=True)
        IL(4, R0)
        QM(4, K1)
        IL(4, R1)
        QM(4, R0)
        QM(4, L1)
        QM(4, R1)
        o_tr(3, (0, 1))
        QM(4, L0, last=True)
        read_unit(4)
        open_unit(5, (6, 7))
        passes = (L1, L0, K0, K1, R0, R1)
        for n, ps in enumerate(passes):
            QM(5, ps, n == 0, n == 5)
        o_tr(4, (2,))
        read_unit(5)
        o_tr(5, (3,))
        o_out(3, work.tile([P, 2, 4 * P], F32, name="agrp", align_bytes=64, bufs=3)[:], th)
        ost = work.tile([P, 2, 2, 2 * P], F32, name="agrp", align_bytes=64, bufs=3)
        o_out(4, ost[:, 0, :, :], th)
        o_out(5, ost[:, 1, :, :], th)
